import numpy as np
import ml_dtypes


def mxq(x, axis, fmt="e4m3"):
    dtype, down = {"e4m3": (ml_dtypes.float8_e4m3fn, 7), "e5m2": (ml_dtypes.float8_e5m2, 14)}[fmt]
    v = np.moveaxis(np.asarray(x, np.float32).astype(ml_dtypes.bfloat16).astype(np.float64), axis, -1)
    blocks = v.reshape(v.shape[:-1] + (-1, 32))
    amax = np.abs(blocks).max(-1, keepdims=True)
    byte = np.maximum(np.where(amax > 0, np.frexp(amax)[1] - 1 + 127, 0) - down, 1)
    scale = np.exp2(byte - 127.0)
    codes = (blocks / scale).astype(np.float32).astype(dtype).astype(np.float64)
    return np.moveaxis((codes * scale).reshape(v.shape), -1, axis)


WIDE = False


def mx_kscale(k):
    if not WIDE:
        return np.ones(k)
    levels = np.array([10, -10, 5, -5, 0])
    a = np.random.permutation(np.resize(levels, k // 512 * 4)).reshape(k // 512, 4)
    idx = np.arange(k)
    return np.exp2(a[idx // 512, idx % 128 // 32])


BF16 = ml_dtypes.bfloat16


def bf(x):
    return np.asarray(x, np.float32).astype(BF16)


def f64(x):
    return np.asarray(x).astype(np.float64)


B, S, IN_DIM, OUT_DIM, R = 4, 128, 2560, 2560, 1024
RB1 = -(-OUT_DIM // R)
PAD = R * RB1 - OUT_DIM
HALF = R // 2
ROPE_BASE = 10000.0


def freqs():
    inv_freq = 1.0 / ROPE_BASE ** (np.arange(0, R, 2) / R)
    emb = np.outer(np.arange(RB1) * 1.0, inv_freq)
    emb = np.concatenate([emb, emb], axis=-1)
    return np.cos(emb), np.sin(emb)


def setup_inputs():
    s = mx_kscale(IN_DIM)
    return {"x": bf(np.random.standard_normal((B, S, IN_DIM)) * s),
            "weight": bf(np.random.standard_normal((OUT_DIM, IN_DIM)) / np.sqrt(IN_DIM) / s),
            "lora_a_weight": bf(np.random.standard_normal((R, R)) * 0.5 / np.sqrt(R))}


def reference(x, weight, lora_a_weight):
    h = mxq(f64(x), 2, "e4m3") @ mxq(f64(weight), 1, "e4m3").T
    cos, sin = freqs()
    z = np.concatenate([h, h[..., :PAD]], axis=-1)
    z = z.reshape(*z.shape[:-1], RB1, R)
    rh = np.concatenate([-z[..., HALF:], z[..., :HALF]], axis=-1)
    z = z * cos + rh * sin
    y = mxq(z, 3, "e4m3") @ mxq(f64(lora_a_weight), 1, "e4m3").T
    y = y.reshape(*y.shape[:-2], RB1 * R)[..., :OUT_DIM]
    return h + y

@@ -1,0 +1,295 @@
+import math
+from contextlib import ExitStack
+
+import concourse.mybir as mybir
+from concourse.masks import make_identity
+
+F32 = mybir.dt.float32
+BF16 = mybir.dt.bfloat16
+I32 = mybir.dt.int32
+U32 = mybir.dt.uint32
+U8 = mybir.dt.uint8
+FP8X4 = mybir.dt.float8_e4m3fn_x4
+ACT = mybir.ActivationFunctionType
+ALU = mybir.AluOpType
+
+P = 128
+PACK = 4
+K_PASS = P * PACK
+TOKENS = 512
+TOKEN_TILES = TOKENS // P
+IN_DIM = 2560
+OUT_DIM = 2560
+RANK = 1024
+ROPE_BASE = 10000.0
+PASSES = IN_DIM // K_PASS
+CHUNK = K_PASS
+CHUNKS = OUT_DIM // CHUNK
+GROUPS = 3
+RANK_PASSES = RANK // K_PASS
+UNITS = CHUNKS * PASSES
+
+FIRST_CHUNK = 2
+LOOKAHEAD = 2
+LORA_TIME = 2
+
+FLOPS = 2 * TOKENS * IN_DIM * OUT_DIM + 2 * TOKENS * RANK * OUT_DIM
+
+
+def chunk_at(time):
+    return (time + FIRST_CHUNK) % CHUNKS
+
+
+def time_of(chunk):
+    return (chunk - FIRST_CHUNK) % CHUNKS
+
+
+def tile_moralinear_pa_kernel(tc, x, weight, lora_a_weight, out):
+    nc = tc.nc
+    x_rows = x.flatten_outer_dims().rearrange("(i q) k -> q i k", q=P)
+    lora_rows = lora_a_weight.rearrange("(i q) r -> q i r", q=P)
+    out_rows = out.flatten_outer_dims()
+
+    with ExitStack() as stack:
+        const = stack.enter_context(tc.tile_pool(name="const", bufs=1))
+        raw_pool = stack.enter_context(tc.tile_pool(name="raw", bufs=3))
+        stage = stack.enter_context(tc.tile_pool(name="stage", bufs=5))
+        unit_pool = stack.enter_context(tc.tile_pool(name="unit", bufs=LOOKAHEAD + 2))
+        keep = stack.enter_context(tc.tile_pool(name="keep", bufs=1))
+        h_pool = stack.enter_context(tc.tile_pool(name="h", bufs=3))
+        z_pool = stack.enter_context(tc.tile_pool(name="z", bufs=3))
+        acc_pool = stack.enter_context(tc.psum_pool(name="acc", bufs=1))
+        work = stack.enter_context(tc.psum_pool(name="work", bufs=4))
+
+        def load_weight_rows(raw, chunk, cols):
+            rows = weight[chunk * CHUNK : (chunk + 1) * CHUNK, :].rearrange(
+                "(u p e) k -> p u e k", u=2, e=2
+            )
+            for u in range(2):
+                nc.sync.dma_start(out=raw[:, 2 * u : 2 * u + 2, cols], in_=rows[:, u, :, cols])
+
+        w_raw = {}
+        x_raw = raw_pool.tile([P, TOKEN_TILES, IN_DIM], BF16, tag="raw")
+        w_raw[0] = raw_pool.tile([P, PACK, IN_DIM], BF16, tag="raw", name="w_raw")
+        for g in range(PASSES):
+            cols = slice(g * K_PASS, (g + 1) * K_PASS)
+            nc.sync.dma_start(out=x_raw[:, :, cols], in_=x_rows[:, :, cols])
+            load_weight_rows(w_raw[0], chunk_at(0), cols)
+        w_raw[1] = raw_pool.tile([P, PACK, IN_DIM], BF16, tag="raw", name="w_raw")
+        load_weight_rows(w_raw[1], chunk_at(1), slice(0, IN_DIM))
+
+        ident = const.tile([P, P], F32)
+        make_identity(nc, ident[:])
+
+        index_i = const.tile([P, PACK], I32)
+        nc.gpsimd.iota(index_i[:], pattern=[[256, 2], [1, 2]], base=0, channel_multiplier=2)
+        index_f = const.tile([P, PACK], F32)
+        nc.vector.tensor_copy(out=index_f[:], in_=index_i[:])
+        inv_freq = const.tile([P, PACK], F32)
+        nc.scalar.activation(
+            out=inv_freq[:], in_=index_f[:], func=ACT.Exp, scale=-math.log(ROPE_BASE) / K_PASS
+        )
+        sin = const.tile([P, GROUPS - 1, PACK], F32)
+        sin_half = const.tile([P, GROUPS - 1, PACK], F32)
+        for n in range(1, GROUPS):
+            nc.scalar.activation(out=sin[:, n - 1, :], in_=inv_freq[:], func=ACT.Sin, scale=1.0 * n)
+            nc.scalar.activation(
+                out=sin_half[:, n - 1, :], in_=inv_freq[:], func=ACT.Sin, scale=0.5 * n
+            )
+        cos = const.tile([P, GROUPS - 1, PACK], F32)
+        nc.vector.tensor_mul(out=cos[:], in0=sin_half[:], in1=sin_half[:])
+        nc.vector.tensor_scalar(
+            out=cos[:], in0=cos[:], scalar1=-2.0, scalar2=1.0, op0=ALU.mult, op1=ALU.add
+        )
+        neg_sin = const.tile([P, GROUPS - 1, PACK], F32)
+        nc.vector.tensor_scalar(
+            out=neg_sin[:], in0=sin[:], scalar1=-1.0, scalar2=None, op0=ALU.mult
+        )
+
+        x_codes = keep.tile([P, PASSES, TOKENS], U32, align_bytes=64)
+        x_scales = keep.tile([P, PASSES, TOKENS], U8, align_bytes=64)
+        a_codes = keep.tile([P, RANK_PASSES, RANK], U32, align_bytes=64)
+        a_scales = keep.tile([P, RANK_PASSES, RANK], U8, align_bytes=64)
+        z_codes = keep.tile([P, GROUPS, RANK_PASSES, TOKENS], U32, align_bytes=64)
+        z_scales = keep.tile([P, GROUPS, RANK_PASSES, TOKENS], U8, align_bytes=64)
+        h_tok = keep.tile([P, TOKEN_TILES, OUT_DIM], F32)
+
+        def transpose_pass(row_tiles, g):
+            grouped = stage.tile([P, CHUNK * PACK], BF16, tag="grouped", align_bytes=64)
+            pairs = grouped[:].bitcast(F32).rearrange("p (c u) -> p c u", u=2)
+            for half in range(2):
+                bank = work.tile([P, 2, 2 * P], F32, tag="work")
+                for u in range(2):
+                    first = (2 * g + u) * P
+                    for j in range(2):
+                        nc.tensor.transpose(
+                            bank[:, u, j * P : (j + 1) * P],
+                            row_tiles[2 * half + j].bitcast(F32)[:, first : first + P],
+                            ident[:],
+                        )
+                dst = pairs[:, 2 * half * P : 2 * (half + 1) * P, :]
+                src = bank[:].rearrange("p u c -> p c u")
+                if half == 1 and g % 2 == 1:
+                    nc.vector.tensor_copy(out=dst, in_=src)
+                else:
+                    nc.scalar.copy(out=dst, in_=src)
+            return grouped
+
+        def quantise(grouped, codes, scales):
+            nc.vector.quantize_mx(out=codes.bitcast(FP8X4), scales=scales, in_=grouped[:])
+
+        def first_stage_pass(acc, codes, scales, g):
+            for t in range(PACK):
+                cols = slice(t * P, (t + 1) * P)
+                nc.tensor.matmul_mx(
+                    out=acc[t][:],
+                    lhsT=codes[:, cols].bitcast(FP8X4),
+                    lhsT_scale=scales[:, cols],
+                    rhs=x_codes[:, g, :].bitcast(FP8X4),
+                    rhs_scale=x_scales[:, g, :],
+                    start=(g == 0),
+                    stop=(g == PASSES - 1),
+                )
+
+        def transpose_h(chunk, i):
+            bank = work.tile([P, PACK, P], F32, tag="work")
+            for t in range(PACK):
+                nc.tensor.transpose(bank[:, t, :], h_t[chunk][:, t, i * P : (i + 1) * P], ident[:])
+            nc.scalar.copy(
+                out=h_tok[:, i, chunk * CHUNK : (chunk + 1) * CHUNK].rearrange(
+                    "q (u p e) -> q u p e", u=2, e=2
+                ),
+                in_=bank[:].rearrange("q (u e) p -> q u p e", u=2),
+            )
+
+        def rotate_slot(chunk, t):
+            mine = h_t[chunk][:, t, :]
+            for n in range(GROUPS):
+                low, high = (2 * n) % CHUNKS, (2 * n + 1) % CHUNKS
+                if n == 0:
+                    for g2 in range(RANK_PASSES):
+                        if chunk == (low, high)[g2]:
+                            if t == 0:
+                                z_rot[(n, g2)] = z_pool.tile([P, PACK, TOKENS], BF16, tag="z", name="z_rot")
+                            nc.scalar.copy(out=z_rot[(n, g2)][:, t, :], in_=mine)
+                elif chunk == low:
+                    if t == 0:
+                        products[n] = keep.tile([P, 2, PACK, TOKENS], F32, tag="products", name="products")
+                    nc.scalar.activation(
+                        out=products[n][:, 0, t, :], in_=mine, func=ACT.Copy, scale=cos[:, n - 1, t : t + 1]
+                    )
+                    nc.scalar.activation(
+                        out=products[n][:, 1, t, :], in_=mine, func=ACT.Copy, scale=sin[:, n - 1, t : t + 1]
+                    )
+                elif chunk == high:
+                    if t == 0:
+                        for g2 in range(RANK_PASSES):
+                            z_rot[(n, g2)] = z_pool.tile([P, PACK, TOKENS], BF16, tag="z", name="z_rot")
+                    nc.vector.scalar_tensor_tensor(
+                        out=z_rot[(n, 0)][:, t, :], in0=mine, scalar=neg_sin[:, n - 1, t : t + 1],
+                        in1=products[n][:, 0, t, :], op0=ALU.mult, op1=ALU.add,
+                    )
+                    nc.vector.scalar_tensor_tensor(
+                        out=z_rot[(n, 1)][:, t, :], in0=mine, scalar=cos[:, n - 1, t : t + 1],
+                        in1=products[n][:, 1, t, :], op0=ALU.mult, op1=ALU.add,
+                    )
+
+        def quantise_rotated(chunk):
+            done = []
+            for n in range(GROUPS):
+                for g2 in range(RANK_PASSES):
+                    last = (2 * n + g2) % CHUNKS if n == 0 else (2 * n + 1) % CHUNKS
+                    if chunk == last:
+                        done.append((n, g2))
+            regrouped = {}
+            for key in done:
+                regrouped[key] = stage.tile([P, TOKENS * PACK], BF16, tag="grouped", name="regrouped", align_bytes=64)
+                nc.vector.tensor_copy(
+                    out=regrouped[key][:].rearrange("p (c i t) -> p c t i", i=4, t=PACK),
+                    in_=z_rot[key][:].rearrange("p t (c i) -> p c t i", i=4),
+                )
+            for n, g2 in done:
+                quantise(regrouped[(n, g2)], z_codes[:, n, g2, :], z_scales[:, n, g2, :])
+
+        def second_stage(n, i):
+            rows = slice(i * P, (i + 1) * P)
+            for chunk in range(2 * n, min(2 * n + 2, CHUNKS)):
+                a_cols = slice((chunk - 2 * n) * CHUNK, (chunk - 2 * n + 1) * CHUNK)
+                y = work.tile([P, CHUNK], F32, tag="work")
+                for g2 in range(RANK_PASSES):
+                    nc.tensor.matmul_mx(
+                        out=y[:],
+                        lhsT=z_codes[:, n, g2, rows].bitcast(FP8X4),
+                        lhsT_scale=z_scales[:, n, g2, rows],
+                        rhs=a_codes[:, g2, a_cols].bitcast(FP8X4),
+                        rhs_scale=a_scales[:, g2, a_cols],
+                        start=(g2 == 0),
+                        stop=(g2 == RANK_PASSES - 1),
+                    )
+                cols = slice(chunk * CHUNK, (chunk + 1) * CHUNK)
+                nc.vector.tensor_add(out=h_tok[:, i, cols], in0=y[:], in1=h_tok[:, i, cols])
+                nc.sync.dma_start(out=out_rows[rows, cols], in_=h_tok[:, i, cols])
+
+        x_grouped, w_grouped, a_grouped = {}, {}, {}
+        w_codes, w_scales = {}, {}
+        h_t, z_rot, products = {}, {}, {}
+        acc = []
+        for step in range(-LOOKAHEAD, (CHUNKS + 2) * PASSES):
+            ahead = step + LOOKAHEAD
+            if ahead < UNITS:
+                time, g = divmod(ahead, PASSES)
+                if time == 0:
+                    x_grouped[g] = transpose_pass([x_raw[:, i, :] for i in range(TOKEN_TILES)], g)
+                w_grouped[ahead] = transpose_pass([w_raw[time][:, t, :] for t in range(PACK)], g)
+                if g == PASSES - 1 and time + 2 < CHUNKS:
+                    w_raw[time + 2] = raw_pool.tile([P, PACK, IN_DIM], BF16, tag="raw", name="w_raw")
+                    load_weight_rows(w_raw[time + 2], chunk_at(time + 2), slice(0, IN_DIM))
+                    if time == 0:
+                        a_raw = raw_pool.tile([P, RANK // P, RANK], BF16, tag="raw")
+                        nc.sync.dma_start(out=a_raw[:], in_=lora_rows)
+
+            c, g = divmod(step, PASSES)
+            if step >= 0 and c >= 1 and c - 1 < CHUNKS and g < TOKEN_TILES:
+                transpose_h(chunk_at(c - 1), g)
+            if step >= 0 and c == LORA_TIME and g < 2 * RANK_PASSES:
+                g2, half = divmod(g, 2)
+                a_grouped[g] = transpose_pass(
+                    [a_raw[:, PACK * half + j, :] for j in range(PACK)], g2
+                )
+
+            ready = ahead - 1
+            if 0 <= ready < UNITS:
+                if ready < PASSES:
+                    quantise(x_grouped[ready], x_codes[:, ready, :], x_scales[:, ready, :])
+                w_codes[ready] = unit_pool.tile([P, CHUNK], U32, tag="codes", name="w_codes", align_bytes=64)
+                w_scales[ready] = unit_pool.tile([P, CHUNK], U8, tag="scales", name="w_scales", align_bytes=64)
+                quantise(w_grouped[ready], w_codes[ready][:], w_scales[ready][:])
+            if step >= 0 and c == LORA_TIME and 1 <= g:
+                g2, half = divmod(g - 1, 2)
+                a_cols = slice(half * CHUNK, (half + 1) * CHUNK)
+                quantise(a_grouped[g - 1], a_codes[:, g2, a_cols], a_scales[:, g2, a_cols])
+
+            if step < 0:
+                continue
+
+            if c >= 1 and c - 1 < CHUNKS:
+                if g < PACK:
+                    rotate_slot(chunk_at(c - 1), g)
+                else:
+                    quantise_rotated(chunk_at(c - 1))
+
+            if c < CHUNKS:
+                if g == 0:
+                    acc = [acc_pool.tile([P, TOKENS], F32, name="acc%d" % t) for t in range(PACK)]
+                first_stage_pass(acc, w_codes[step], w_scales[step], g)
+                if g == PASSES - 1:
+                    h_t[chunk_at(c)] = h_pool.tile([P, PACK, TOKENS], F32, tag="h_t", name="h_t")
+                    for t in range(PACK):
+                        if t % 2 == 0:
+                            nc.scalar.copy(out=h_t[chunk_at(c)][:, t, :], in_=acc[t][:])
+                        else:
+                            nc.vector.tensor_copy(out=h_t[chunk_at(c)][:, t, :], in_=acc[t][:])
+
+            for n in range(GROUPS):
+                if c == time_of((2 * n + 1) % CHUNKS) + 2 and g < TOKEN_TILES:
+                    second_stage(n, g)

@@ -60,6 +60,7 @@ def tile_moralinear_pa_kernel(tc, x, weight, lora_a_weight, out):
         z_pool = stack.enter_context(tc.tile_pool(name="z", bufs=3))
         acc_pool = stack.enter_context(tc.psum_pool(name="acc", bufs=1))
         work = stack.enter_context(tc.psum_pool(name="work", bufs=4))
+        stack.enter_context(tc.manual_schedule())
 
         def load_weight_rows(raw, chunk, cols):
             rows = weight[chunk * CHUNK : (chunk + 1) * CHUNK, :].rearrange(

@@ -29,19 +29,21 @@ GROUPS = 3
 RANK_PASSES = RANK // K_PASS
 UNITS = CHUNKS * PASSES
 
-FIRST_CHUNK = 2
+ORDER = (2, 3, 0, 4, 1)
 LOOKAHEAD = 2
+LOAD_AHEAD = 8
+RAW_UNITS = 16
 LORA_TIME = 2
 
 FLOPS = 2 * TOKENS * IN_DIM * OUT_DIM + 2 * TOKENS * RANK * OUT_DIM
 
 
 def chunk_at(time):
-    return (time + FIRST_CHUNK) % CHUNKS
+    return ORDER[time]
 
 
 def time_of(chunk):
-    return (chunk - FIRST_CHUNK) % CHUNKS
+    return ORDER.index(chunk)
 
 
 def tile_moralinear_pa_kernel(tc, x, weight, lora_a_weight, out):
@@ -52,32 +54,45 @@ def tile_moralinear_pa_kernel(tc, x, weight, lora_a_weight, out):
 
     with ExitStack() as stack:
         const = stack.enter_context(tc.tile_pool(name="const", bufs=1))
-        raw_pool = stack.enter_context(tc.tile_pool(name="raw", bufs=3))
+        raw_pool = stack.enter_context(tc.tile_pool(name="raw", bufs=RAW_UNITS))
         stage = stack.enter_context(tc.tile_pool(name="stage", bufs=5))
         unit_pool = stack.enter_context(tc.tile_pool(name="unit", bufs=LOOKAHEAD + 2))
         keep = stack.enter_context(tc.tile_pool(name="keep", bufs=1))
-        h_pool = stack.enter_context(tc.tile_pool(name="h", bufs=3))
-        z_pool = stack.enter_context(tc.tile_pool(name="z", bufs=3))
+        h_pool = stack.enter_context(tc.tile_pool(name="h", bufs=2))
+        z_pool = stack.enter_context(tc.tile_pool(name="z", bufs=2))
         acc_pool = stack.enter_context(tc.psum_pool(name="acc", bufs=1))
         work = stack.enter_context(tc.psum_pool(name="work", bufs=4))
         stack.enter_context(tc.manual_schedule())
 
-        def load_weight_rows(raw, chunk, cols):
-            rows = weight[chunk * CHUNK : (chunk + 1) * CHUNK, :].rearrange(
-                "(u p e) k -> p u e k", u=2, e=2
-            )
-            for u in range(2):
-                nc.sync.dma_start(out=raw[:, 2 * u : 2 * u + 2, cols], in_=rows[:, u, :, cols])
+        def load_x_unit(g):
+            raw = raw_pool.tile([P, PACK, K_PASS], BF16, tag="raw")
+            nc.sync.dma_start(out=raw[:], in_=x_rows[:, :, g * K_PASS : (g + 1) * K_PASS])
+            return raw
 
-        w_raw = {}
-        x_raw = raw_pool.tile([P, TOKEN_TILES, IN_DIM], BF16, tag="raw")
-        w_raw[0] = raw_pool.tile([P, PACK, IN_DIM], BF16, tag="raw", name="w_raw")
-        for g in range(PASSES):
-            cols = slice(g * K_PASS, (g + 1) * K_PASS)
-            nc.sync.dma_start(out=x_raw[:, :, cols], in_=x_rows[:, :, cols])
-            load_weight_rows(w_raw[0], chunk_at(0), cols)
-        w_raw[1] = raw_pool.tile([P, PACK, IN_DIM], BF16, tag="raw", name="w_raw")
-        load_weight_rows(w_raw[1], chunk_at(1), slice(0, IN_DIM))
+        def load_lora_unit(g2, half):
+            raw = raw_pool.tile([P, PACK, K_PASS], BF16, tag="raw")
+            nc.sync.dma_start(
+                out=raw[:],
+                in_=lora_rows[:, PACK * half : PACK * (half + 1), g2 * K_PASS : (g2 + 1) * K_PASS],
+            )
+            return raw
+
+        def load_weight_unit(unit):
+            time, g = divmod(unit, PASSES)
+            first_row = chunk_at(time) * CHUNK
+            rows = weight[first_row : first_row + CHUNK, :].rearrange("(u p e) k -> p u e k", u=2, e=2)
+            raw = raw_pool.tile([P, PACK, K_PASS], BF16, tag="raw")
+            for u in range(2):
+                nc.sync.dma_start(
+                    out=raw[:, 2 * u : 2 * u + 2, :], in_=rows[:, u, :, g * K_PASS : (g + 1) * K_PASS]
+                )
+            return raw
+
+        x_raw, w_raw, a_raw = {}, {}, {}
+        for unit in range(LOAD_AHEAD):
+            if unit < PASSES:
+                x_raw[unit] = load_x_unit(unit)
+            w_raw[unit] = load_weight_unit(unit)
 
         ident = const.tile([P, P], F32)
         make_identity(nc, ident[:])
@@ -115,25 +130,21 @@ def tile_moralinear_pa_kernel(tc, x, weight, lora_a_weight, out):
         z_scales = keep.tile([P, GROUPS, RANK_PASSES, TOKENS], U8, align_bytes=64)
         h_tok = keep.tile([P, TOKEN_TILES, OUT_DIM], F32)
 
-        def transpose_pass(row_tiles, g):
+        def transpose_unit(raw):
             grouped = stage.tile([P, CHUNK * PACK], BF16, tag="grouped", align_bytes=64)
             pairs = grouped[:].bitcast(F32).rearrange("p (c u) -> p c u", u=2)
             for half in range(2):
                 bank = work.tile([P, 2, 2 * P], F32, tag="work")
                 for u in range(2):
-                    first = (2 * g + u) * P
                     for j in range(2):
                         nc.tensor.transpose(
                             bank[:, u, j * P : (j + 1) * P],
-                            row_tiles[2 * half + j].bitcast(F32)[:, first : first + P],
+                            raw[:, 2 * half + j, :].bitcast(F32)[:, u * P : (u + 1) * P],
                             ident[:],
                         )
                 dst = pairs[:, 2 * half * P : 2 * (half + 1) * P, :]
                 src = bank[:].rearrange("p u c -> p c u")
-                if half == 1 and g % 2 == 1:
-                    nc.vector.tensor_copy(out=dst, in_=src)
-                else:
-                    nc.scalar.copy(out=dst, in_=src)
+                nc.scalar.copy(out=dst, in_=src)
             return grouped
 
         def quantise(grouped, codes, scales):
@@ -172,44 +183,51 @@ def tile_moralinear_pa_kernel(tc, x, weight, lora_a_weight, out):
                         if chunk == (low, high)[g2]:
                             if t == 0:
                                 z_rot[(n, g2)] = z_pool.tile([P, PACK, TOKENS], BF16, tag="z", name="z_rot")
-                            nc.scalar.copy(out=z_rot[(n, g2)][:, t, :], in_=mine)
-                elif chunk == low:
-                    if t == 0:
-                        products[n] = keep.tile([P, 2, PACK, TOKENS], F32, tag="products", name="products")
-                    nc.scalar.activation(
-                        out=products[n][:, 0, t, :], in_=mine, func=ACT.Copy, scale=cos[:, n - 1, t : t + 1]
-                    )
-                    nc.scalar.activation(
-                        out=products[n][:, 1, t, :], in_=mine, func=ACT.Copy, scale=sin[:, n - 1, t : t + 1]
-                    )
-                elif chunk == high:
-                    if t == 0:
+                            if t % 2 == 0:
+                                nc.scalar.copy(out=z_rot[(n, g2)][:, t, :], in_=mine)
+                            else:
+                                nc.vector.tensor_copy(out=z_rot[(n, g2)][:, t, :], in_=mine)
+                elif chunk in (low, high):
+                    factor = ((cos, neg_sin), (sin, cos))
+                    half = (low, high).index(chunk)
+                    if time_of(chunk) == min(time_of(low), time_of(high)):
+                        if t == 0:
+                            products[n] = keep.tile([P, 2, PACK, TOKENS], F32, tag="products", name="products")
                         for g2 in range(RANK_PASSES):
-                            z_rot[(n, g2)] = z_pool.tile([P, PACK, TOKENS], BF16, tag="z", name="z_rot")
-                    nc.vector.scalar_tensor_tensor(
-                        out=z_rot[(n, 0)][:, t, :], in0=mine, scalar=neg_sin[:, n - 1, t : t + 1],
-                        in1=products[n][:, 0, t, :], op0=ALU.mult, op1=ALU.add,
-                    )
-                    nc.vector.scalar_tensor_tensor(
-                        out=z_rot[(n, 1)][:, t, :], in0=mine, scalar=cos[:, n - 1, t : t + 1],
-                        in1=products[n][:, 1, t, :], op0=ALU.mult, op1=ALU.add,
-                    )
+                            nc.vector.tensor_scalar(
+                                out=products[n][:, g2, t, :], in0=mine,
+                                scalar1=factor[g2][half][:, n - 1, t : t + 1], scalar2=None, op0=ALU.mult,
+                            )
+                    else:
+                        for g2 in range(RANK_PASSES):
+                            if t == 0:
+                                z_rot[(n, g2)] = z_pool.tile([P, PACK, TOKENS], BF16, tag="z", name="z_rot")
+                            nc.vector.scalar_tensor_tensor(
+                                out=z_rot[(n, g2)][:, t, :], in0=mine,
+                                scalar=factor[g2][half][:, n - 1, t : t + 1],
+                                in1=products[n][:, g2, t, :], op0=ALU.mult, op1=ALU.add,
+                            )
 
-        def quantise_rotated(chunk):
+        def completed_by(chunk):
             done = []
-            for n in range(GROUPS):
+            for n in range(GROUPS - 1, -1, -1):
                 for g2 in range(RANK_PASSES):
-                    last = (2 * n + g2) % CHUNKS if n == 0 else (2 * n + 1) % CHUNKS
+                    low, high = (2 * n) % CHUNKS, (2 * n + 1) % CHUNKS
+                    last = (low, high)[g2] if n == 0 else max(low, high, key=time_of)
                     if chunk == last:
                         done.append((n, g2))
-            regrouped = {}
-            for key in done:
+            return done
+
+        def regroup_rotated(chunk):
+            for key in completed_by(chunk):
                 regrouped[key] = stage.tile([P, TOKENS * PACK], BF16, tag="grouped", name="regrouped", align_bytes=64)
                 nc.vector.tensor_copy(
                     out=regrouped[key][:].rearrange("p (c i t) -> p c t i", i=4, t=PACK),
                     in_=z_rot[key][:].rearrange("p t (c i) -> p c t i", i=4),
                 )
-            for n, g2 in done:
+
+        def quantise_rotated(chunk):
+            for n, g2 in completed_by(chunk):
                 quantise(regrouped[(n, g2)], z_codes[:, n, g2, :], z_scales[:, n, g2, :])
 
         def second_stage(n, i):
@@ -233,31 +251,18 @@ def tile_moralinear_pa_kernel(tc, x, weight, lora_a_weight, out):
 
         x_grouped, w_grouped, a_grouped = {}, {}, {}
         w_codes, w_scales = {}, {}
-        h_t, z_rot, products = {}, {}, {}
+        h_t, z_rot, products, regrouped = {}, {}, {}, {}
         acc = []
-        for step in range(-LOOKAHEAD, (CHUNKS + 2) * PASSES):
+        for step in range(-LOOKAHEAD, (CHUNKS + 1) * PASSES):
             ahead = step + LOOKAHEAD
             if ahead < UNITS:
-                time, g = divmod(ahead, PASSES)
-                if time == 0:
-                    x_grouped[g] = transpose_pass([x_raw[:, i, :] for i in range(TOKEN_TILES)], g)
-                w_grouped[ahead] = transpose_pass([w_raw[time][:, t, :] for t in range(PACK)], g)
-                if g == PASSES - 1 and time + 2 < CHUNKS:
-                    w_raw[time + 2] = raw_pool.tile([P, PACK, IN_DIM], BF16, tag="raw", name="w_raw")
-                    load_weight_rows(w_raw[time + 2], chunk_at(time + 2), slice(0, IN_DIM))
-                    if time == 0:
-                        a_raw = raw_pool.tile([P, RANK // P, RANK], BF16, tag="raw")
-                        nc.sync.dma_start(out=a_raw[:], in_=lora_rows)
+                if ahead < PASSES:
+                    x_grouped[ahead] = transpose_unit(x_raw[ahead])
+                w_grouped[ahead] = transpose_unit(w_raw[ahead])
+                if ahead + LOAD_AHEAD < UNITS:
+                    w_raw[ahead + LOAD_AHEAD] = load_weight_unit(ahead + LOAD_AHEAD)
 
             c, g = divmod(step, PASSES)
-            if step >= 0 and c >= 1 and c - 1 < CHUNKS and g < TOKEN_TILES:
-                transpose_h(chunk_at(c - 1), g)
-            if step >= 0 and c == LORA_TIME and g < 2 * RANK_PASSES:
-                g2, half = divmod(g, 2)
-                a_grouped[g] = transpose_pass(
-                    [a_raw[:, PACK * half + j, :] for j in range(PACK)], g2
-                )
-
             ready = ahead - 1
             if 0 <= ready < UNITS:
                 if ready < PASSES:
@@ -265,6 +270,23 @@ def tile_moralinear_pa_kernel(tc, x, weight, lora_a_weight, out):
                 w_codes[ready] = unit_pool.tile([P, CHUNK], U32, tag="codes", name="w_codes", align_bytes=64)
                 w_scales[ready] = unit_pool.tile([P, CHUNK], U8, tag="scales", name="w_scales", align_bytes=64)
                 quantise(w_grouped[ready], w_codes[ready][:], w_scales[ready][:])
+            if step >= 0 and c >= 1 and c - 1 < CHUNKS:
+                if g < 2:
+                    rotate_slot(chunk_at(c - 1), 2 * g)
+                    rotate_slot(chunk_at(c - 1), 2 * g + 1)
+                elif g == 2:
+                    regroup_rotated(chunk_at(c - 1))
+                elif g == 3:
+                    quantise_rotated(chunk_at(c - 1))
+
+            if step >= 0 and c >= 1 and c - 1 < CHUNKS and g < TOKEN_TILES:
+                transpose_h(chunk_at(c - 1), g)
+            if step >= 0 and c == LORA_TIME - 1 and g < 2 * RANK_PASSES:
+                g2, half = divmod(g, 2)
+                a_raw[g] = load_lora_unit(g2, half)
+            if step >= 0 and c == LORA_TIME and g < 2 * RANK_PASSES:
+                a_grouped[g] = transpose_unit(a_raw[g])
+
             if step >= 0 and c == LORA_TIME and 1 <= g:
                 g2, half = divmod(g - 1, 2)
                 a_cols = slice(half * CHUNK, (half + 1) * CHUNK)
@@ -272,12 +294,6 @@ def tile_moralinear_pa_kernel(tc, x, weight, lora_a_weight, out):
 
             if step < 0:
                 continue
-
-            if c >= 1 and c - 1 < CHUNKS:
-                if g < PACK:
-                    rotate_slot(chunk_at(c - 1), g)
-                else:
-                    quantise_rotated(chunk_at(c - 1))
 
             if c < CHUNKS:
                 if g == 0:
@@ -292,5 +308,6 @@ def tile_moralinear_pa_kernel(tc, x, weight, lora_a_weight, out):
                             nc.vector.tensor_copy(out=h_t[chunk_at(c)][:, t, :], in_=acc[t][:])
 
             for n in range(GROUPS):
-                if c == time_of((2 * n + 1) % CHUNKS) + 2 and g < TOKEN_TILES:
-                    second_stage(n, g)
+                if c == max(time_of((2 * n) % CHUNKS), time_of((2 * n + 1) % CHUNKS)) + 1 and g == PASSES - 1:
+                    for i in range(TOKEN_TILES):
+                        second_stage(n, i)

@@ -33,6 +33,11 @@ ORDER = (2, 3, 0, 4, 1)
 LOOKAHEAD = 2
 LOAD_AHEAD = 8
 RAW_UNITS = 16
+REGROUP_S = ()
+DOUBLE = 16
+UB = 8
+SB = 6
+HT = 1
 LORA_TIME = 2
 
 FLOPS = 2 * TOKENS * IN_DIM * OUT_DIM + 2 * TOKENS * RANK * OUT_DIM
@@ -55,8 +60,8 @@ def tile_moralinear_pa_kernel(tc, x, weight, lora_a_weight, out):
     with ExitStack() as stack:
         const = stack.enter_context(tc.tile_pool(name="const", bufs=1))
         raw_pool = stack.enter_context(tc.tile_pool(name="raw", bufs=RAW_UNITS))
-        stage = stack.enter_context(tc.tile_pool(name="stage", bufs=5))
-        unit_pool = stack.enter_context(tc.tile_pool(name="unit", bufs=LOOKAHEAD + 2))
+        stage = stack.enter_context(tc.tile_pool(name="stage", bufs=SB))
+        unit_pool = stack.enter_context(tc.tile_pool(name="unit", bufs=UB))
         keep = stack.enter_context(tc.tile_pool(name="keep", bufs=1))
         h_pool = stack.enter_context(tc.tile_pool(name="h", bufs=2))
         z_pool = stack.enter_context(tc.tile_pool(name="z", bufs=2))
@@ -82,6 +87,10 @@ def tile_moralinear_pa_kernel(tc, x, weight, lora_a_weight, out):
             first_row = chunk_at(time) * CHUNK
             rows = weight[first_row : first_row + CHUNK, :].rearrange("(u p e) k -> p u e k", u=2, e=2)
             raw = raw_pool.tile([P, PACK, K_PASS], BF16, tag="raw")
+            if time == CHUNKS - 1:
+                natural = weight[first_row : first_row + CHUNK, :].rearrange("(j q) k -> q j k", q=P)
+                nc.sync.dma_start(out=raw[:], in_=natural[:, :, g * K_PASS : (g + 1) * K_PASS])
+                return raw
             for u in range(2):
                 nc.sync.dma_start(
                     out=raw[:, 2 * u : 2 * u + 2, :], in_=rows[:, u, :, g * K_PASS : (g + 1) * K_PASS]
@@ -221,7 +230,8 @@ def tile_moralinear_pa_kernel(tc, x, weight, lora_a_weight, out):
         def regroup_rotated(chunk):
             for key in completed_by(chunk):
                 regrouped[key] = stage.tile([P, TOKENS * PACK], BF16, tag="grouped", name="regrouped", align_bytes=64)
-                nc.vector.tensor_copy(
+                move = nc.scalar.copy if key in REGROUP_S else nc.vector.tensor_copy
+                move(
                     out=regrouped[key][:].rearrange("p (c i t) -> p c t i", i=4, t=PACK),
                     in_=z_rot[key][:].rearrange("p t (c i) -> p c t i", i=4),
                 )
@@ -229,6 +239,50 @@ def tile_moralinear_pa_kernel(tc, x, weight, lora_a_weight, out):
         def quantise_rotated(chunk):
             for n, g2 in completed_by(chunk):
                 quantise(regrouped[(n, g2)], z_codes[:, n, g2, :], z_scales[:, n, g2, :])
+
+        last_acc, last_codes, last_scales, last_z, last_grouped = {}, {}, {}, {}, {}
+
+        def zr_codes(n, g2, i):
+            return last_codes[i][:] if (n, g2) == (0, 1) else z_codes[:, n, g2, i * P : (i + 1) * P]
+
+        def zr_scales(n, g2, i):
+            return last_scales[i][:] if (n, g2) == (0, 1) else z_scales[:, n, g2, i * P : (i + 1) * P]
+
+        def last_chunk(i):
+            acc = acc_pool.tile([P, CHUNK], F32, name="acc%d" % i)
+            for g in range(PASSES):
+                unit = UNITS - PASSES + g
+                nc.tensor.matmul_mx(
+                    out=acc[:],
+                    lhsT=x_codes[:, g, i * P : (i + 1) * P].bitcast(FP8X4),
+                    lhsT_scale=x_scales[:, g, i * P : (i + 1) * P],
+                    rhs=w_codes[unit][:].bitcast(FP8X4),
+                    rhs_scale=w_scales[unit][:],
+                    start=(g == 0),
+                    stop=(g == PASSES - 1),
+                )
+            last_z[i] = z_pool.tile([P, CHUNK], BF16, tag="last_z", bufs=TOKEN_TILES, name="last_z")
+            nc.scalar.copy(out=last_z[i][:], in_=acc[:])
+            last_acc[i] = acc
+
+        def keep_last(i):
+            first = chunk_at(CHUNKS - 1) * CHUNK
+            nc.scalar.copy(out=h_tok[:, i, first : first + CHUNK], in_=last_acc[i][:])
+
+        def transpose_last(i):
+            last_grouped[i] = stage.tile([P, P * PACK], BF16, tag="last", bufs=2, name="last_grouped", align_bytes=64)
+            bank = work.tile([P, 2, P], F32, tag="work")
+            for u in range(2):
+                nc.tensor.transpose(bank[:, u, :], last_z[i][:].bitcast(F32)[:, u * P : (u + 1) * P], ident[:])
+            nc.scalar.copy(
+                out=last_grouped[i][:].bitcast(F32).rearrange("p (c u) -> p c u", u=2),
+                in_=bank[:].rearrange("p u c -> p c u"),
+            )
+
+        def quantise_last(i):
+            last_codes[i] = keep.tile([P, P], U32, name="last_codes%d" % i, align_bytes=64)
+            last_scales[i] = keep.tile([P, P], U8, name="last_scales%d" % i, align_bytes=64)
+            quantise(last_grouped[i], last_codes[i][:], last_scales[i][:])
 
         def second_stage(n, i):
             rows = slice(i * P, (i + 1) * P)
@@ -238,8 +292,8 @@ def tile_moralinear_pa_kernel(tc, x, weight, lora_a_weight, out):
                 for g2 in range(RANK_PASSES):
                     nc.tensor.matmul_mx(
                         out=y[:],
-                        lhsT=z_codes[:, n, g2, rows].bitcast(FP8X4),
-                        lhsT_scale=z_scales[:, n, g2, rows],
+                        lhsT=zr_codes(n, g2, i).bitcast(FP8X4),
+                        lhsT_scale=zr_scales(n, g2, i),
                         rhs=a_codes[:, g2, a_cols].bitcast(FP8X4),
                         rhs_scale=a_scales[:, g2, a_cols],
                         start=(g2 == 0),
@@ -253,23 +307,26 @@ def tile_moralinear_pa_kernel(tc, x, weight, lora_a_weight, out):
         w_codes, w_scales = {}, {}
         h_t, z_rot, products, regrouped = {}, {}, {}, {}
         acc = []
-        for step in range(-LOOKAHEAD, (CHUNKS + 1) * PASSES):
-            ahead = step + LOOKAHEAD
-            if ahead < UNITS:
-                if ahead < PASSES:
-                    x_grouped[ahead] = transpose_unit(x_raw[ahead])
-                w_grouped[ahead] = transpose_unit(w_raw[ahead])
-                if ahead + LOAD_AHEAD < UNITS:
-                    w_raw[ahead + LOAD_AHEAD] = load_weight_unit(ahead + LOAD_AHEAD)
-
+        fresh, turned = [], 0
+        for step in range(-LOOKAHEAD, UNITS - PASSES):
             c, g = divmod(step, PASSES)
-            ready = ahead - 1
-            if 0 <= ready < UNITS:
-                if ready < PASSES:
-                    quantise(x_grouped[ready], x_codes[:, ready, :], x_scales[:, ready, :])
-                w_codes[ready] = unit_pool.tile([P, CHUNK], U32, tag="codes", name="w_codes", align_bytes=64)
-                w_scales[ready] = unit_pool.tile([P, CHUNK], U8, tag="scales", name="w_scales", align_bytes=64)
-                quantise(w_grouped[ready], w_codes[ready][:], w_scales[ready][:])
+            ready = fresh
+            many = 2 if step >= DOUBLE else 1
+            fresh = list(range(turned, min(turned + many, UNITS)))
+            turned += len(fresh)
+            for unit in fresh:
+                if unit < PASSES:
+                    x_grouped[unit] = transpose_unit(x_raw[unit])
+                w_grouped[unit] = transpose_unit(w_raw[unit])
+                if unit + LOAD_AHEAD < UNITS:
+                    w_raw[unit + LOAD_AHEAD] = load_weight_unit(unit + LOAD_AHEAD)
+
+            for unit in ready:
+                if unit < PASSES:
+                    quantise(x_grouped[unit], x_codes[:, unit, :], x_scales[:, unit, :])
+                w_codes[unit] = unit_pool.tile([P, CHUNK], U32, tag="codes", name="w_codes", align_bytes=64)
+                w_scales[unit] = unit_pool.tile([P, CHUNK], U8, tag="scales", name="w_scales", align_bytes=64)
+                quantise(w_grouped[unit], w_codes[unit][:], w_scales[unit][:])
             if step >= 0 and c >= 1 and c - 1 < CHUNKS:
                 if g < 2:
                     rotate_slot(chunk_at(c - 1), 2 * g)
@@ -279,8 +336,8 @@ def tile_moralinear_pa_kernel(tc, x, weight, lora_a_weight, out):
                 elif g == 3:
                     quantise_rotated(chunk_at(c - 1))
 
-            if step >= 0 and c >= 1 and c - 1 < CHUNKS and g < TOKEN_TILES:
-                transpose_h(chunk_at(c - 1), g)
+            if step >= 0 and c >= 1 and HT <= g < HT + TOKEN_TILES:
+                transpose_h(chunk_at(c - 1), g - HT)
             if step >= 0 and c == LORA_TIME - 1 and g < 2 * RANK_PASSES:
                 g2, half = divmod(g, 2)
                 a_raw[g] = load_lora_unit(g2, half)
@@ -295,7 +352,7 @@ def tile_moralinear_pa_kernel(tc, x, weight, lora_a_weight, out):
             if step < 0:
                 continue
 
-            if c < CHUNKS:
+            if c < CHUNKS - 1:
                 if g == 0:
                     acc = [acc_pool.tile([P, TOKENS], F32, name="acc%d" % t) for t in range(PACK)]
                 first_stage_pass(acc, w_codes[step], w_scales[step], g)
@@ -307,7 +364,45 @@ def tile_moralinear_pa_kernel(tc, x, weight, lora_a_weight, out):
                         else:
                             nc.vector.tensor_copy(out=h_t[chunk_at(c)][:, t, :], in_=acc[t][:])
 
-            for n in range(GROUPS):
-                if c == max(time_of((2 * n) % CHUNKS), time_of((2 * n + 1) % CHUNKS)) + 1 and g == PASSES - 1:
-                    for i in range(TOKEN_TILES):
-                        second_stage(n, i)
+            if c == CHUNKS - 2 and g < TOKEN_TILES:
+                second_stage(1, g)
+
+        before = chunk_at(CHUNKS - 2)
+        for unit in fresh:
+            w_codes[unit] = unit_pool.tile([P, CHUNK], U32, tag="codes", name="w_codes", align_bytes=64)
+            w_scales[unit] = unit_pool.tile([P, CHUNK], U8, tag="scales", name="w_scales", align_bytes=64)
+            quantise(w_grouped[unit], w_codes[unit][:], w_scales[unit][:])
+        rotate_slot(before, 0)
+        rotate_slot(before, 1)
+        last_chunk(0)
+        transpose_h(before, 0)
+        transpose_h(before, 1)
+        rotate_slot(before, 2)
+        rotate_slot(before, 3)
+        last_chunk(1)
+        transpose_last(0)
+        regroup_rotated(before)
+        last_chunk(2)
+        transpose_last(1)
+        quantise_last(0)
+        transpose_h(before, 2)
+        transpose_h(before, 3)
+        last_chunk(3)
+        quantise_rotated(before)
+        quantise_last(1)
+        transpose_last(2)
+        keep_last(0)
+        second_stage(0, 0)
+        transpose_last(3)
+        keep_last(1)
+        keep_last(2)
+        keep_last(3)
+        quantise_last(2)
+        second_stage(0, 1)
+        quantise_last(3)
+        second_stage(2, 0)
+        second_stage(2, 1)
+        second_stage(0, 2)
+        second_stage(2, 2)
+        second_stage(0, 3)
+        second_stage(2, 3)

@@ -33,12 +33,17 @@ ORDER = (2, 3, 0, 4, 1)
 LOOKAHEAD = 2
 LOAD_AHEAD = 8
 RAW_UNITS = 16
-REGROUP_S = ()
-DOUBLE = 16
-UB = 8
+DOUBLE = 14
+UB = 9
 SB = 6
 HT = 1
 LORA_TIME = 2
+REGROUP_S = ()
+CATCH = 3
+HX = "SS"
+HW = "SV"
+VU = ()
+HS = (3,)
 
 FLOPS = 2 * TOKENS * IN_DIM * OUT_DIM + 2 * TOKENS * RANK * OUT_DIM
 
@@ -139,7 +144,7 @@ def tile_moralinear_pa_kernel(tc, x, weight, lora_a_weight, out):
         z_scales = keep.tile([P, GROUPS, RANK_PASSES, TOKENS], U8, align_bytes=64)
         h_tok = keep.tile([P, TOKEN_TILES, OUT_DIM], F32)
 
-        def transpose_unit(raw):
+        def transpose_unit(raw, engines="SS"):
             grouped = stage.tile([P, CHUNK * PACK], BF16, tag="grouped", align_bytes=64)
             pairs = grouped[:].bitcast(F32).rearrange("p (c u) -> p c u", u=2)
             for half in range(2):
@@ -153,7 +158,10 @@ def tile_moralinear_pa_kernel(tc, x, weight, lora_a_weight, out):
                         )
                 dst = pairs[:, 2 * half * P : 2 * (half + 1) * P, :]
                 src = bank[:].rearrange("p u c -> p c u")
-                nc.scalar.copy(out=dst, in_=src)
+                if engines[half] == "S":
+                    nc.scalar.copy(out=dst, in_=src)
+                else:
+                    nc.vector.tensor_copy(out=dst, in_=src)
             return grouped
 
         def quantise(grouped, codes, scales):
@@ -306,27 +314,33 @@ def tile_moralinear_pa_kernel(tc, x, weight, lora_a_weight, out):
         x_grouped, w_grouped, a_grouped = {}, {}, {}
         w_codes, w_scales = {}, {}
         h_t, z_rot, products, regrouped = {}, {}, {}, {}
+        def quantise_unit(unit):
+            if unit < PASSES:
+                quantise(x_grouped[unit], x_codes[:, unit, :], x_scales[:, unit, :])
+            w_codes[unit] = unit_pool.tile([P, CHUNK], U32, tag="codes", name="w_codes", align_bytes=64)
+            w_scales[unit] = unit_pool.tile([P, CHUNK], U8, tag="scales", name="w_scales", align_bytes=64)
+            quantise(w_grouped[unit], w_codes[unit][:], w_scales[unit][:])
+
         acc = []
         fresh, turned = [], 0
-        for step in range(-LOOKAHEAD, UNITS - PASSES):
+        for step in range(-1, UNITS - PASSES):
             c, g = divmod(step, PASSES)
             ready = fresh
-            many = 2 if step >= DOUBLE else 1
+            many = 2 if step >= DOUBLE or step == CATCH else 1
             fresh = list(range(turned, min(turned + many, UNITS)))
             turned += len(fresh)
             for unit in fresh:
                 if unit < PASSES:
-                    x_grouped[unit] = transpose_unit(x_raw[unit])
-                w_grouped[unit] = transpose_unit(w_raw[unit])
+                    x_grouped[unit] = transpose_unit(x_raw[unit], HX)
+                w_grouped[unit] = transpose_unit(w_raw[unit], HW if unit < PASSES else "SV" if unit in VU else "SS")
+                if unit < CATCH + 1:
+                    quantise_unit(unit)
                 if unit + LOAD_AHEAD < UNITS:
                     w_raw[unit + LOAD_AHEAD] = load_weight_unit(unit + LOAD_AHEAD)
 
             for unit in ready:
-                if unit < PASSES:
-                    quantise(x_grouped[unit], x_codes[:, unit, :], x_scales[:, unit, :])
-                w_codes[unit] = unit_pool.tile([P, CHUNK], U32, tag="codes", name="w_codes", align_bytes=64)
-                w_scales[unit] = unit_pool.tile([P, CHUNK], U8, tag="scales", name="w_scales", align_bytes=64)
-                quantise(w_grouped[unit], w_codes[unit][:], w_scales[unit][:])
+                if unit >= CATCH + 1:
+                    quantise_unit(unit)
             if step >= 0 and c >= 1 and c - 1 < CHUNKS:
                 if g < 2:
                     rotate_slot(chunk_at(c - 1), 2 * g)
@@ -359,7 +373,7 @@ def tile_moralinear_pa_kernel(tc, x, weight, lora_a_weight, out):
                 if g == PASSES - 1:
                     h_t[chunk_at(c)] = h_pool.tile([P, PACK, TOKENS], F32, tag="h_t", name="h_t")
                     for t in range(PACK):
-                        if t % 2 == 0:
+                        if t % 2 == 0 or c in HS:
                             nc.scalar.copy(out=h_t[chunk_at(c)][:, t, :], in_=acc[t][:])
                         else:
                             nc.vector.tensor_copy(out=h_t[chunk_at(c)][:, t, :], in_=acc[t][:])
@@ -369,9 +383,7 @@ def tile_moralinear_pa_kernel(tc, x, weight, lora_a_weight, out):
 
         before = chunk_at(CHUNKS - 2)
         for unit in fresh:
-            w_codes[unit] = unit_pool.tile([P, CHUNK], U32, tag="codes", name="w_codes", align_bytes=64)
-            w_scales[unit] = unit_pool.tile([P, CHUNK], U8, tag="scales", name="w_scales", align_bytes=64)
-            quantise(w_grouped[unit], w_codes[unit][:], w_scales[unit][:])
+            quantise_unit(unit)
         rotate_slot(before, 0)
         rotate_slot(before, 1)
         last_chunk(0)
@@ -380,19 +392,19 @@ def tile_moralinear_pa_kernel(tc, x, weight, lora_a_weight, out):
         rotate_slot(before, 2)
         rotate_slot(before, 3)
         last_chunk(1)
-        transpose_last(0)
-        regroup_rotated(before)
         last_chunk(2)
+        transpose_last(0)
         transpose_last(1)
-        quantise_last(0)
+        regroup_rotated(before)
         transpose_h(before, 2)
         transpose_h(before, 3)
+        quantise_last(0)
         last_chunk(3)
         quantise_rotated(before)
         quantise_last(1)
-        transpose_last(2)
         keep_last(0)
         second_stage(0, 0)
+        transpose_last(2)
         transpose_last(3)
         keep_last(1)
         keep_last(2)

@@ -32,7 +32,7 @@ UNITS = CHUNKS * PASSES
 ORDER = (2, 3, 0, 4, 1)
 LOOKAHEAD = 2
 LOAD_AHEAD = 8
-RAW_UNITS = 16
+RAW_UNITS = 15
 DOUBLE = 14
 UB = 9
 SB = 6
@@ -40,10 +40,11 @@ HT = 1
 LORA_TIME = 2
 REGROUP_S = ()
 CATCH = 3
-HX = "SS"
-HW = "SV"
-VU = ()
+HX = "SV"
+HW = "VS"
+VU = (8, 9, 10, 11)
 HS = (3,)
+PAIRS = (6, 8, 18)
 
 FLOPS = 2 * TOKENS * IN_DIM * OUT_DIM + 2 * TOKENS * RANK * OUT_DIM
 
@@ -136,12 +137,12 @@ def tile_moralinear_pa_kernel(tc, x, weight, lora_a_weight, out):
             out=neg_sin[:], in0=sin[:], scalar1=-1.0, scalar2=None, op0=ALU.mult
         )
 
-        x_codes = keep.tile([P, PASSES, TOKENS], U32, align_bytes=64)
-        x_scales = keep.tile([P, PASSES, TOKENS], U8, align_bytes=64)
-        a_codes = keep.tile([P, RANK_PASSES, RANK], U32, align_bytes=64)
-        a_scales = keep.tile([P, RANK_PASSES, RANK], U8, align_bytes=64)
-        z_codes = keep.tile([P, GROUPS, RANK_PASSES, TOKENS], U32, align_bytes=64)
-        z_scales = keep.tile([P, GROUPS, RANK_PASSES, TOKENS], U8, align_bytes=64)
+        x_codes = keep.tile([P, PASSES, TOKENS], U32, align_bytes=256)
+        x_scales = keep.tile([P, PASSES, TOKENS], U8, align_bytes=256)
+        a_codes = keep.tile([P, RANK_PASSES, RANK], U32, align_bytes=256)
+        a_scales = keep.tile([P, RANK_PASSES, RANK], U8, align_bytes=256)
+        z_codes = keep.tile([P, GROUPS, RANK_PASSES, TOKENS], U32, align_bytes=256)
+        z_scales = keep.tile([P, GROUPS, RANK_PASSES, TOKENS], U8, align_bytes=256)
         h_tok = keep.tile([P, TOKEN_TILES, OUT_DIM], F32)
 
         def transpose_unit(raw, engines="SS"):
@@ -288,8 +289,8 @@ def tile_moralinear_pa_kernel(tc, x, weight, lora_a_weight, out):
             )
 
         def quantise_last(i):
-            last_codes[i] = keep.tile([P, P], U32, name="last_codes%d" % i, align_bytes=64)
-            last_scales[i] = keep.tile([P, P], U8, name="last_scales%d" % i, align_bytes=64)
+            last_codes[i] = keep.tile([P, P], U32, name="last_codes%d" % i, align_bytes=256)
+            last_scales[i] = keep.tile([P, P], U8, name="last_scales%d" % i, align_bytes=256)
             quantise(last_grouped[i], last_codes[i][:], last_scales[i][:])
 
         def second_stage(n, i):
@@ -317,18 +318,18 @@ def tile_moralinear_pa_kernel(tc, x, weight, lora_a_weight, out):
         def quantise_unit(unit):
             if unit < PASSES:
                 quantise(x_grouped[unit], x_codes[:, unit, :], x_scales[:, unit, :])
-            w_codes[unit] = unit_pool.tile([P, CHUNK], U32, tag="codes", name="w_codes", align_bytes=64)
-            w_scales[unit] = unit_pool.tile([P, CHUNK], U8, tag="scales", name="w_scales", align_bytes=64)
+            w_codes[unit] = unit_pool.tile([P, CHUNK], U32, tag="codes", name="w_codes", align_bytes=256)
+            w_scales[unit] = unit_pool.tile([P, CHUNK], U8, tag="scales", name="w_scales", align_bytes=256)
             quantise(w_grouped[unit], w_codes[unit][:], w_scales[unit][:])
 
-        acc = []
-        fresh, turned = [], 0
-        for step in range(-1, UNITS - PASSES):
+        state = {"fresh": [], "turned": 0}
+
+        def turn_part(step):
             c, g = divmod(step, PASSES)
-            ready = fresh
+            ready = state["fresh"]
             many = 2 if step >= DOUBLE or step == CATCH else 1
-            fresh = list(range(turned, min(turned + many, UNITS)))
-            turned += len(fresh)
+            fresh = list(range(state["turned"], min(state["turned"] + many, UNITS)))
+            state["fresh"], state["turned"] = fresh, state["turned"] + len(fresh)
             for unit in fresh:
                 if unit < PASSES:
                     x_grouped[unit] = transpose_unit(x_raw[unit], HX)
@@ -363,24 +364,35 @@ def tile_moralinear_pa_kernel(tc, x, weight, lora_a_weight, out):
                 a_cols = slice(half * CHUNK, (half + 1) * CHUNK)
                 quantise(a_grouped[g - 1], a_codes[:, g2, a_cols], a_scales[:, g2, a_cols])
 
-            if step < 0:
-                continue
+        accs = {}
 
+        def pass_part(step):
+            c, g = divmod(step, PASSES)
             if c < CHUNKS - 1:
                 if g == 0:
-                    acc = [acc_pool.tile([P, TOKENS], F32, name="acc%d" % t) for t in range(PACK)]
-                first_stage_pass(acc, w_codes[step], w_scales[step], g)
+                    accs[c] = [acc_pool.tile([P, TOKENS], F32, name="acc%d" % t) for t in range(PACK)]
+                first_stage_pass(accs[c], w_codes[step], w_scales[step], g)
                 if g == PASSES - 1:
                     h_t[chunk_at(c)] = h_pool.tile([P, PACK, TOKENS], F32, tag="h_t", name="h_t")
                     for t in range(PACK):
                         if t % 2 == 0 or c in HS:
-                            nc.scalar.copy(out=h_t[chunk_at(c)][:, t, :], in_=acc[t][:])
+                            nc.scalar.copy(out=h_t[chunk_at(c)][:, t, :], in_=accs[c][t][:])
                         else:
-                            nc.vector.tensor_copy(out=h_t[chunk_at(c)][:, t, :], in_=acc[t][:])
+                            nc.vector.tensor_copy(out=h_t[chunk_at(c)][:, t, :], in_=accs[c][t][:])
 
             if c == CHUNKS - 2 and g < TOKEN_TILES:
                 second_stage(1, g)
 
+        step = -1
+        while step < UNITS - PASSES:
+            many = 2 if step in PAIRS else 1
+            for s in range(step, step + many):
+                turn_part(s)
+            for s in range(step, step + many):
+                if s >= 0:
+                    pass_part(s)
+            step += many
+        fresh = state["fresh"]
         before = chunk_at(CHUNKS - 2)
         for unit in fresh:
             quantise_unit(unit)

@@ -32,19 +32,25 @@ UNITS = CHUNKS * PASSES
 ORDER = (2, 3, 0, 4, 1)
 LOOKAHEAD = 2
 LOAD_AHEAD = 8
-RAW_UNITS = 15
-DOUBLE = 14
-UB = 9
+RAW_UNITS = 14
+UB = 11
 SB = 6
-HT = 1
-LORA_TIME = 2
 REGROUP_S = ()
-CATCH = 3
+
 HX = "SV"
 HW = "VS"
-VU = (8, 9, 10, 11)
-HS = (3,)
-PAIRS = (6, 8, 18)
+HE = "SS"
+VE = ("", "SS", "SS", "SS")
+KV = (0, 1, 2)
+LATE = 0
+HD = 0
+HP = 1
+LL = (5, 6, 7, 8)
+LT = (9, 10, 12, 14)
+EARLY = 4
+ROUNDS = 4
+SHARE = ((), (2, 1, 1, 1), (2, 1, 1, 1), (2, 2, 1, 0))
+HEAD = (((0,), ()), ((1,), (0,)), ((2,), (1,)), ((3,), (2,)), ((4, 5), (3,)), ((6, 7), (4,)), ((8, 9), ()))
 
 FLOPS = 2 * TOKENS * IN_DIM * OUT_DIM + 2 * TOKENS * RANK * OUT_DIM
 
@@ -71,8 +77,7 @@ def tile_moralinear_pa_kernel(tc, x, weight, lora_a_weight, out):
         keep = stack.enter_context(tc.tile_pool(name="keep", bufs=1))
         h_pool = stack.enter_context(tc.tile_pool(name="h", bufs=2))
         z_pool = stack.enter_context(tc.tile_pool(name="z", bufs=2))
-        acc_pool = stack.enter_context(tc.psum_pool(name="acc", bufs=1))
-        work = stack.enter_context(tc.psum_pool(name="work", bufs=4))
+        psum = stack.enter_context(tc.psum_pool(name="psum", bufs=8))
         stack.enter_context(tc.manual_schedule())
 
         def load_x_unit(g):
@@ -149,7 +154,7 @@ def tile_moralinear_pa_kernel(tc, x, weight, lora_a_weight, out):
             grouped = stage.tile([P, CHUNK * PACK], BF16, tag="grouped", align_bytes=64)
             pairs = grouped[:].bitcast(F32).rearrange("p (c u) -> p c u", u=2)
             for half in range(2):
-                bank = work.tile([P, 2, 2 * P], F32, tag="work")
+                bank = psum.tile([P, 2, 2 * P], F32, tag="bank", name="bank")
                 for u in range(2):
                     for j in range(2):
                         nc.tensor.transpose(
@@ -168,21 +173,34 @@ def tile_moralinear_pa_kernel(tc, x, weight, lora_a_weight, out):
         def quantise(grouped, codes, scales):
             nc.vector.quantize_mx(out=codes.bitcast(FP8X4), scales=scales, in_=grouped[:])
 
-        def first_stage_pass(acc, codes, scales, g):
-            for t in range(PACK):
-                cols = slice(t * P, (t + 1) * P)
-                nc.tensor.matmul_mx(
-                    out=acc[t][:],
-                    lhsT=codes[:, cols].bitcast(FP8X4),
-                    lhsT_scale=scales[:, cols],
-                    rhs=x_codes[:, g, :].bitcast(FP8X4),
-                    rhs_scale=x_scales[:, g, :],
-                    start=(g == 0),
-                    stop=(g == PASSES - 1),
-                )
+        accs = {}
+
+        def first_stage_pass(time, t, g):
+            if g == 0:
+                accs[t] = psum.tile([P, TOKENS], F32, tag="bank", name="acc")
+            unit = time * PASSES + g
+            cols = slice(t * P, (t + 1) * P)
+            nc.tensor.matmul_mx(
+                out=accs[t][:],
+                lhsT=w_codes[unit][:, cols].bitcast(FP8X4),
+                lhsT_scale=w_scales[unit][:, cols],
+                rhs=x_codes[:, g, :].bitcast(FP8X4),
+                rhs_scale=x_scales[:, g, :],
+                start=(g == 0),
+                stop=(g == PASSES - 1),
+            )
+
+        def keep_slot(time, t, engine):
+            if t == 0:
+                h_t[chunk_at(time)] = h_pool.tile([P, PACK, TOKENS], F32, tag="h_t", name="h_t")
+            kept = h_t[chunk_at(time)][:, t, :]
+            if engine == "S":
+                nc.scalar.copy(out=kept, in_=accs[t][:])
+            else:
+                nc.vector.tensor_copy(out=kept, in_=accs[t][:])
 
         def transpose_h(chunk, i):
-            bank = work.tile([P, PACK, P], F32, tag="work")
+            bank = psum.tile([P, PACK, P], F32, tag="bank", name="bank")
             for t in range(PACK):
                 nc.tensor.transpose(bank[:, t, :], h_t[chunk][:, t, i * P : (i + 1) * P], ident[:])
             nc.scalar.copy(
@@ -258,7 +276,7 @@ def tile_moralinear_pa_kernel(tc, x, weight, lora_a_weight, out):
             return last_scales[i][:] if (n, g2) == (0, 1) else z_scales[:, n, g2, i * P : (i + 1) * P]
 
         def last_chunk(i):
-            acc = acc_pool.tile([P, CHUNK], F32, name="acc%d" % i)
+            acc = psum.tile([P, CHUNK], F32, tag="bank", name="acc")
             for g in range(PASSES):
                 unit = UNITS - PASSES + g
                 nc.tensor.matmul_mx(
@@ -280,7 +298,7 @@ def tile_moralinear_pa_kernel(tc, x, weight, lora_a_weight, out):
 
         def transpose_last(i):
             last_grouped[i] = stage.tile([P, P * PACK], BF16, tag="last", bufs=2, name="last_grouped", align_bytes=64)
-            bank = work.tile([P, 2, P], F32, tag="work")
+            bank = psum.tile([P, 2, P], F32, tag="bank", name="bank")
             for u in range(2):
                 nc.tensor.transpose(bank[:, u, :], last_z[i][:].bitcast(F32)[:, u * P : (u + 1) * P], ident[:])
             nc.scalar.copy(
@@ -297,7 +315,7 @@ def tile_moralinear_pa_kernel(tc, x, weight, lora_a_weight, out):
             rows = slice(i * P, (i + 1) * P)
             for chunk in range(2 * n, min(2 * n + 2, CHUNKS)):
                 a_cols = slice((chunk - 2 * n) * CHUNK, (chunk - 2 * n + 1) * CHUNK)
-                y = work.tile([P, CHUNK], F32, tag="work")
+                y = psum.tile([P, CHUNK], F32, tag="bank", name="y")
                 for g2 in range(RANK_PASSES):
                     nc.tensor.matmul_mx(
                         out=y[:],
@@ -315,6 +333,7 @@ def tile_moralinear_pa_kernel(tc, x, weight, lora_a_weight, out):
         x_grouped, w_grouped, a_grouped = {}, {}, {}
         w_codes, w_scales = {}, {}
         h_t, z_rot, products, regrouped = {}, {}, {}, {}
+
         def quantise_unit(unit):
             if unit < PASSES:
                 quantise(x_grouped[unit], x_codes[:, unit, :], x_scales[:, unit, :])
@@ -322,111 +341,127 @@ def tile_moralinear_pa_kernel(tc, x, weight, lora_a_weight, out):
             w_scales[unit] = unit_pool.tile([P, CHUNK], U8, tag="scales", name="w_scales", align_bytes=256)
             quantise(w_grouped[unit], w_codes[unit][:], w_scales[unit][:])
 
-        state = {"fresh": [], "turned": 0}
+        def turn_unit(unit, engines):
+            if unit < PASSES:
+                x_grouped[unit] = transpose_unit(x_raw[unit], HX)
+            w_grouped[unit] = transpose_unit(w_raw[unit], HW if unit < PASSES else engines)
+            if unit + LOAD_AHEAD < UNITS:
+                w_raw[unit + LOAD_AHEAD] = load_weight_unit(unit + LOAD_AHEAD)
 
-        def turn_part(step):
-            c, g = divmod(step, PASSES)
-            ready = state["fresh"]
-            many = 2 if step >= DOUBLE or step == CATCH else 1
-            fresh = list(range(state["turned"], min(state["turned"] + many, UNITS)))
-            state["fresh"], state["turned"] = fresh, state["turned"] + len(fresh)
+        def load_lora(v):
+            a_raw[v] = load_lora_unit(v // 2, v % 2)
+
+        def turn_lora(v):
+            a_grouped[v] = transpose_unit(a_raw[v], "SS")
+
+        def quantise_lora(v):
+            a_cols = slice(v % 2 * CHUNK, (v % 2 + 1) * CHUNK)
+            quantise(a_grouped[v], a_codes[:, v // 2, a_cols], a_scales[:, v // 2, a_cols])
+
+        due = {}
+
+        def at(k, step, f, *arguments):
+            due.setdefault((k, step), []).append((f, arguments))
+
+        def run(k, step):
+            for f, arguments in due.get((k, step), []):
+                f(*arguments)
+
+        def finish_slot(time, t, k):
+            keep_slot(time, t, "V" if t % 2 == 1 and time in KV else "S")
+            chunk = chunk_at(time)
+            when = k + 1 if time else k + 1 + t // 2
+            if time < 3 or t < 4 - LATE:
+                at(when, "vector", rotate_slot, chunk, t)
+            if t == PACK - 1 and time < 3:
+                last = when
+                at(last + 1, "vector", regroup_rotated, chunk)
+                at(last + 2, "vector", quantise_rotated, chunk)
+                for i in range(TOKEN_TILES):
+                    at(k + 1 + HD + i // HP, "turn", transpose_h, chunk, i)
+
+        for v in range(4):
+            at(LL[v], "load", load_lora, v)
+            at(LT[v], "turn", turn_lora, v)
+            at(LT[v] + 1, "vector", quantise_lora, v)
+        k = 0
+        fresh = []
+        for units, passes in HEAD:
+            run(k, "load")
+            for unit in units:
+                turn_unit(unit, HE)
+                if unit < EARLY:
+                    quantise_unit(unit)
             for unit in fresh:
-                if unit < PASSES:
-                    x_grouped[unit] = transpose_unit(x_raw[unit], HX)
-                w_grouped[unit] = transpose_unit(w_raw[unit], HW if unit < PASSES else "SV" if unit in VU else "SS")
-                if unit < CATCH + 1:
+                if unit >= EARLY:
                     quantise_unit(unit)
-                if unit + LOAD_AHEAD < UNITS:
-                    w_raw[unit + LOAD_AHEAD] = load_weight_unit(unit + LOAD_AHEAD)
-
-            for unit in ready:
-                if unit >= CATCH + 1:
-                    quantise_unit(unit)
-            if step >= 0 and c >= 1 and c - 1 < CHUNKS:
-                if g < 2:
-                    rotate_slot(chunk_at(c - 1), 2 * g)
-                    rotate_slot(chunk_at(c - 1), 2 * g + 1)
-                elif g == 2:
-                    regroup_rotated(chunk_at(c - 1))
-                elif g == 3:
-                    quantise_rotated(chunk_at(c - 1))
-
-            if step >= 0 and c >= 1 and HT <= g < HT + TOKEN_TILES:
-                transpose_h(chunk_at(c - 1), g - HT)
-            if step >= 0 and c == LORA_TIME - 1 and g < 2 * RANK_PASSES:
-                g2, half = divmod(g, 2)
-                a_raw[g] = load_lora_unit(g2, half)
-            if step >= 0 and c == LORA_TIME and g < 2 * RANK_PASSES:
-                a_grouped[g] = transpose_unit(a_raw[g])
-
-            if step >= 0 and c == LORA_TIME and 1 <= g:
-                g2, half = divmod(g - 1, 2)
-                a_cols = slice(half * CHUNK, (half + 1) * CHUNK)
-                quantise(a_grouped[g - 1], a_codes[:, g2, a_cols], a_scales[:, g2, a_cols])
-
-        accs = {}
-
-        def pass_part(step):
-            c, g = divmod(step, PASSES)
-            if c < CHUNKS - 1:
-                if g == 0:
-                    accs[c] = [acc_pool.tile([P, TOKENS], F32, name="acc%d" % t) for t in range(PACK)]
-                first_stage_pass(accs[c], w_codes[step], w_scales[step], g)
+            fresh = units
+            run(k, "vector")
+            run(k, "turn")
+            for g in passes:
+                for t in range(PACK):
+                    first_stage_pass(0, t, g)
                 if g == PASSES - 1:
-                    h_t[chunk_at(c)] = h_pool.tile([P, PACK, TOKENS], F32, tag="h_t", name="h_t")
                     for t in range(PACK):
-                        if t % 2 == 0 or c in HS:
-                            nc.scalar.copy(out=h_t[chunk_at(c)][:, t, :], in_=accs[c][t][:])
-                        else:
-                            nc.vector.tensor_copy(out=h_t[chunk_at(c)][:, t, :], in_=accs[c][t][:])
+                        finish_slot(0, t, k)
+            k += 1
+        turned = 2 * PASSES
+        for time in range(1, CHUNKS - 1):
+            for r in range(ROUNDS):
+                run(k, "load")
+                many = SHARE[time][r]
+                units = range(turned, turned + many)
+                turned += many
+                for unit in units:
+                    turn_unit(unit, VE[time])
+                for unit in fresh:
+                    quantise_unit(unit)
+                fresh = units
+                run(k, "vector")
+                run(k, "turn")
+                for t in range(r * PACK // ROUNDS, (r + 1) * PACK // ROUNDS):
+                    for g in range(PASSES):
+                        first_stage_pass(time, t, g)
+                    finish_slot(time, t, k)
+                run(k, "passes")
+                if time == CHUNKS - 2:
+                    for i in range(r * TOKEN_TILES // ROUNDS, (r + 1) * TOKEN_TILES // ROUNDS):
+                        second_stage(1, i)
+                k += 1
 
-            if c == CHUNKS - 2 and g < TOKEN_TILES:
-                second_stage(1, g)
-
-        step = -1
-        while step < UNITS - PASSES:
-            many = 2 if step in PAIRS else 1
-            for s in range(step, step + many):
-                turn_part(s)
-            for s in range(step, step + many):
-                if s >= 0:
-                    pass_part(s)
-            step += many
-        fresh = state["fresh"]
         before = chunk_at(CHUNKS - 2)
         for unit in fresh:
             quantise_unit(unit)
-        rotate_slot(before, 0)
-        rotate_slot(before, 1)
+        run(k, "vector")
+        for t in range(4 - LATE, 4):
+            rotate_slot(before, t)
         last_chunk(0)
+        last_chunk(1)
         transpose_h(before, 0)
         transpose_h(before, 1)
-        rotate_slot(before, 2)
-        rotate_slot(before, 3)
-        last_chunk(1)
-        last_chunk(2)
         transpose_last(0)
-        transpose_last(1)
         regroup_rotated(before)
+        last_chunk(2)
         transpose_h(before, 2)
         transpose_h(before, 3)
+        transpose_last(1)
+        keep_last(0)
         quantise_last(0)
         last_chunk(3)
         quantise_rotated(before)
         quantise_last(1)
-        keep_last(0)
-        second_stage(0, 0)
         transpose_last(2)
-        transpose_last(3)
         keep_last(1)
-        keep_last(2)
-        keep_last(3)
+        second_stage(0, 0)
+        second_stage(2, 0)
         quantise_last(2)
         second_stage(0, 1)
-        quantise_last(3)
-        second_stage(2, 0)
+        transpose_last(3)
+        keep_last(2)
+        keep_last(3)
         second_stage(2, 1)
-        second_stage(0, 2)
+        quantise_last(3)
         second_stage(2, 2)
-        second_stage(0, 3)
+        second_stage(0, 2)
         second_stage(2, 3)
+        second_stage(0, 3)

import math
from contextlib import ExitStack

import concourse.mybir as mybir
from concourse.masks import make_identity

F32 = mybir.dt.float32
BF16 = mybir.dt.bfloat16
I32 = mybir.dt.int32
U32 = mybir.dt.uint32
U8 = mybir.dt.uint8
FP8X4 = mybir.dt.float8_e4m3fn_x4
ACT = mybir.ActivationFunctionType
ALU = mybir.AluOpType

P = 128
PACK = 4
K_PASS = P * PACK
TOKENS = 512
TOKEN_TILES = TOKENS // P
IN_DIM = 2560
OUT_DIM = 2560
RANK = 1024
ROPE_BASE = 10000.0
PASSES = IN_DIM // K_PASS
CHUNK = K_PASS
CHUNKS = OUT_DIM // CHUNK
GROUPS = 3
RANK_PASSES = RANK // K_PASS
UNITS = CHUNKS * PASSES

ORDER = (2, 3, 0, 4, 1)
LOOKAHEAD = 2
LOAD_AHEAD = 8
RAW_UNITS = 14
UB = 11
SB = 6
REGROUP_S = ()

HX = "SV"
HW = "VS"
HE = "SS"
VE = ("", "SS", "SS", "SS")
KV = (0, 1, 2)
LATE = 0
HD = 0
HP = 1
LL = (5, 6, 7, 8)
LT = (9, 10, 12, 14)
EARLY = 4
ROUNDS = 4
SHARE = ((), (2, 1, 1, 1), (2, 1, 1, 1), (2, 2, 1, 0))
HEAD = (((0,), ()), ((1,), (0,)), ((2,), (1,)), ((3,), (2,)), ((4, 5), (3,)), ((6, 7), (4,)), ((8, 9), ()))

FLOPS = 2 * TOKENS * IN_DIM * OUT_DIM + 2 * TOKENS * RANK * OUT_DIM


def chunk_at(time):
    return ORDER[time]


def time_of(chunk):
    return ORDER.index(chunk)


def tile_moralinear_pa_kernel(tc, x, weight, lora_a_weight, out):
    nc = tc.nc
    x_rows = x.flatten_outer_dims().rearrange("(i q) k -> q i k", q=P)
    lora_rows = lora_a_weight.rearrange("(i q) r -> q i r", q=P)
    out_rows = out.flatten_outer_dims()

    with ExitStack() as stack:
        const = stack.enter_context(tc.tile_pool(name="const", bufs=1))
        raw_pool = stack.enter_context(tc.tile_pool(name="raw", bufs=RAW_UNITS))
        stage = stack.enter_context(tc.tile_pool(name="stage", bufs=SB))
        unit_pool = stack.enter_context(tc.tile_pool(name="unit", bufs=UB))
        keep = stack.enter_context(tc.tile_pool(name="keep", bufs=1))
        h_pool = stack.enter_context(tc.tile_pool(name="h", bufs=2))
        z_pool = stack.enter_context(tc.tile_pool(name="z", bufs=2))
        psum = stack.enter_context(tc.psum_pool(name="psum", bufs=8))
        stack.enter_context(tc.manual_schedule())

        def load_x_unit(g):
            raw = raw_pool.tile([P, PACK, K_PASS], BF16, tag="raw")
            nc.sync.dma_start(out=raw[:], in_=x_rows[:, :, g * K_PASS : (g + 1) * K_PASS])
            return raw

        def load_lora_unit(g2, half):
            raw = raw_pool.tile([P, PACK, K_PASS], BF16, tag="raw")
            nc.sync.dma_start(
                out=raw[:],
                in_=lora_rows[:, PACK * half : PACK * (half + 1), g2 * K_PASS : (g2 + 1) * K_PASS],
            )
            return raw

        def load_weight_unit(unit):
            time, g = divmod(unit, PASSES)
            first_row = chunk_at(time) * CHUNK
            rows = weight[first_row : first_row + CHUNK, :].rearrange("(u p e) k -> p u e k", u=2, e=2)
            raw = raw_pool.tile([P, PACK, K_PASS], BF16, tag="raw")
            if time == CHUNKS - 1:
                natural = weight[first_row : first_row + CHUNK, :].rearrange("(j q) k -> q j k", q=P)
                nc.sync.dma_start(out=raw[:], in_=natural[:, :, g * K_PASS : (g + 1) * K_PASS])
                return raw
            for u in range(2):
                nc.sync.dma_start(
                    out=raw[:, 2 * u : 2 * u + 2, :], in_=rows[:, u, :, g * K_PASS : (g + 1) * K_PASS]
                )
            return raw

        x_raw, w_raw, a_raw = {}, {}, {}
        for unit in range(LOAD_AHEAD):
            if unit < PASSES:
                x_raw[unit] = load_x_unit(unit)
            w_raw[unit] = load_weight_unit(unit)

        ident = const.tile([P, P], F32)
        make_identity(nc, ident[:])

        index_i = const.tile([P, PACK], I32)
        nc.gpsimd.iota(index_i[:], pattern=[[256, 2], [1, 2]], base=0, channel_multiplier=2)
        index_f = const.tile([P, PACK], F32)
        nc.vector.tensor_copy(out=index_f[:], in_=index_i[:])
        inv_freq = const.tile([P, PACK], F32)
        nc.scalar.activation(
            out=inv_freq[:], in_=index_f[:], func=ACT.Exp, scale=-math.log(ROPE_BASE) / K_PASS
        )
        sin = const.tile([P, GROUPS - 1, PACK], F32)
        sin_half = const.tile([P, GROUPS - 1, PACK], F32)
        for n in range(1, GROUPS):
            nc.scalar.activation(out=sin[:, n - 1, :], in_=inv_freq[:], func=ACT.Sin, scale=1.0 * n)
            nc.scalar.activation(
                out=sin_half[:, n - 1, :], in_=inv_freq[:], func=ACT.Sin, scale=0.5 * n
            )
        cos = const.tile([P, GROUPS - 1, PACK], F32)
        nc.vector.tensor_mul(out=cos[:], in0=sin_half[:], in1=sin_half[:])
        nc.vector.tensor_scalar(
            out=cos[:], in0=cos[:], scalar1=-2.0, scalar2=1.0, op0=ALU.mult, op1=ALU.add
        )
        neg_sin = const.tile([P, GROUPS - 1, PACK], F32)
        nc.vector.tensor_scalar(
            out=neg_sin[:], in0=sin[:], scalar1=-1.0, scalar2=None, op0=ALU.mult
        )

        x_codes = keep.tile([P, PASSES, TOKENS], U32, align_bytes=256)
        x_scales = keep.tile([P, PASSES, TOKENS], U8, align_bytes=256)
        a_codes = keep.tile([P, RANK_PASSES, RANK], U32, align_bytes=256)
        a_scales = keep.tile([P, RANK_PASSES, RANK], U8, align_bytes=256)
        z_codes = keep.tile([P, GROUPS, RANK_PASSES, TOKENS], U32, align_bytes=256)
        z_scales = keep.tile([P, GROUPS, RANK_PASSES, TOKENS], U8, align_bytes=256)
        h_tok = keep.tile([P, TOKEN_TILES, OUT_DIM], F32)

        def transpose_unit(raw, engines="SS"):
            grouped = stage.tile([P, CHUNK * PACK], BF16, tag="grouped", align_bytes=64)
            pairs = grouped[:].bitcast(F32).rearrange("p (c u) -> p c u", u=2)
            for half in range(2):
                bank = psum.tile([P, 2, 2 * P], F32, tag="bank", name="bank")
                for u in range(2):
                    for j in range(2):
                        nc.tensor.transpose(
                            bank[:, u, j * P : (j + 1) * P],
                            raw[:, 2 * half + j, :].bitcast(F32)[:, u * P : (u + 1) * P],
                            ident[:],
                        )
                dst = pairs[:, 2 * half * P : 2 * (half + 1) * P, :]
                src = bank[:].rearrange("p u c -> p c u")
                if engines[half] == "S":
                    nc.scalar.copy(out=dst, in_=src)
                else:
                    nc.vector.tensor_copy(out=dst, in_=src)
            return grouped

        def quantise(grouped, codes, scales):
            nc.vector.quantize_mx(out=codes.bitcast(FP8X4), scales=scales, in_=grouped[:])

        accs = {}

        def first_stage_pass(time, t, g):
            if g == 0:
                accs[t] = psum.tile([P, TOKENS], F32, tag="bank", name="acc")
            unit = time * PASSES + g
            cols = slice(t * P, (t + 1) * P)
            nc.tensor.matmul_mx(
                out=accs[t][:],
                lhsT=w_codes[unit][:, cols].bitcast(FP8X4),
                lhsT_scale=w_scales[unit][:, cols],
                rhs=x_codes[:, g, :].bitcast(FP8X4),
                rhs_scale=x_scales[:, g, :],
                start=(g == 0),
                stop=(g == PASSES - 1),
            )

        def keep_slot(time, t, engine):
            if t == 0:
                h_t[chunk_at(time)] = h_pool.tile([P, PACK, TOKENS], F32, tag="h_t", name="h_t")
            kept = h_t[chunk_at(time)][:, t, :]
            if engine == "S":
                nc.scalar.copy(out=kept, in_=accs[t][:])
            else:
                nc.vector.tensor_copy(out=kept, in_=accs[t][:])

        def transpose_h(chunk, i):
            bank = psum.tile([P, PACK, P], F32, tag="bank", name="bank")
            for t in range(PACK):
                nc.tensor.transpose(bank[:, t, :], h_t[chunk][:, t, i * P : (i + 1) * P], ident[:])
            nc.scalar.copy(
                out=h_tok[:, i, chunk * CHUNK : (chunk + 1) * CHUNK].rearrange(
                    "q (u p e) -> q u p e", u=2, e=2
                ),
                in_=bank[:].rearrange("q (u e) p -> q u p e", u=2),
            )

        def rotate_slot(chunk, t):
            mine = h_t[chunk][:, t, :]
            for n in range(GROUPS):
                low, high = (2 * n) % CHUNKS, (2 * n + 1) % CHUNKS
                if n == 0:
                    for g2 in range(RANK_PASSES):
                        if chunk == (low, high)[g2]:
                            if t == 0:
                                z_rot[(n, g2)] = z_pool.tile([P, PACK, TOKENS], BF16, tag="z", name="z_rot")
                            if t % 2 == 0:
                                nc.scalar.copy(out=z_rot[(n, g2)][:, t, :], in_=mine)
                            else:
                                nc.vector.tensor_copy(out=z_rot[(n, g2)][:, t, :], in_=mine)
                elif chunk in (low, high):
                    factor = ((cos, neg_sin), (sin, cos))
                    half = (low, high).index(chunk)
                    if time_of(chunk) == min(time_of(low), time_of(high)):
                        if t == 0:
                            products[n] = keep.tile([P, 2, PACK, TOKENS], F32, tag="products", name="products")
                        for g2 in range(RANK_PASSES):
                            nc.vector.tensor_scalar(
                                out=products[n][:, g2, t, :], in0=mine,
                                scalar1=factor[g2][half][:, n - 1, t : t + 1], scalar2=None, op0=ALU.mult,
                            )
                    else:
                        for g2 in range(RANK_PASSES):
                            if t == 0:
                                z_rot[(n, g2)] = z_pool.tile([P, PACK, TOKENS], BF16, tag="z", name="z_rot")
                            nc.vector.scalar_tensor_tensor(
                                out=z_rot[(n, g2)][:, t, :], in0=mine,
                                scalar=factor[g2][half][:, n - 1, t : t + 1],
                                in1=products[n][:, g2, t, :], op0=ALU.mult, op1=ALU.add,
                            )

        def completed_by(chunk):
            done = []
            for n in range(GROUPS - 1, -1, -1):
                for g2 in range(RANK_PASSES):
                    low, high = (2 * n) % CHUNKS, (2 * n + 1) % CHUNKS
                    last = (low, high)[g2] if n == 0 else max(low, high, key=time_of)
                    if chunk == last:
                        done.append((n, g2))
            return done

        def regroup_rotated(chunk):
            for key in completed_by(chunk):
                regrouped[key] = stage.tile([P, TOKENS * PACK], BF16, tag="grouped", name="regrouped", align_bytes=64)
                move = nc.scalar.copy if key in REGROUP_S else nc.vector.tensor_copy
                move(
                    out=regrouped[key][:].rearrange("p (c i t) -> p c t i", i=4, t=PACK),
                    in_=z_rot[key][:].rearrange("p t (c i) -> p c t i", i=4),
                )

        def quantise_rotated(chunk):
            for n, g2 in completed_by(chunk):
                quantise(regrouped[(n, g2)], z_codes[:, n, g2, :], z_scales[:, n, g2, :])

        last_acc, last_codes, last_scales, last_z, last_grouped = {}, {}, {}, {}, {}

        def zr_codes(n, g2, i):
            return last_codes[i][:] if (n, g2) == (0, 1) else z_codes[:, n, g2, i * P : (i + 1) * P]

        def zr_scales(n, g2, i):
            return last_scales[i][:] if (n, g2) == (0, 1) else z_scales[:, n, g2, i * P : (i + 1) * P]

        def last_chunk(i):
            acc = psum.tile([P, CHUNK], F32, tag="bank", name="acc")
            for g in range(PASSES):
                unit = UNITS - PASSES + g
                nc.tensor.matmul_mx(
                    out=acc[:],
                    lhsT=x_codes[:, g, i * P : (i + 1) * P].bitcast(FP8X4),
                    lhsT_scale=x_scales[:, g, i * P : (i + 1) * P],
                    rhs=w_codes[unit][:].bitcast(FP8X4),
                    rhs_scale=w_scales[unit][:],
                    start=(g == 0),
                    stop=(g == PASSES - 1),
                )
            last_z[i] = z_pool.tile([P, CHUNK], BF16, tag="last_z", bufs=TOKEN_TILES, name="last_z")
            nc.scalar.copy(out=last_z[i][:], in_=acc[:])
            last_acc[i] = acc

        def keep_last(i):
            first = chunk_at(CHUNKS - 1) * CHUNK
            nc.scalar.copy(out=h_tok[:, i, first : first + CHUNK], in_=last_acc[i][:])

        def transpose_last(i):
            last_grouped[i] = stage.tile([P, P * PACK], BF16, tag="last", bufs=2, name="last_grouped", align_bytes=64)
            bank = psum.tile([P, 2, P], F32, tag="bank", name="bank")
            for u in range(2):
                nc.tensor.transpose(bank[:, u, :], last_z[i][:].bitcast(F32)[:, u * P : (u + 1) * P], ident[:])
            nc.scalar.copy(
                out=last_grouped[i][:].bitcast(F32).rearrange("p (c u) -> p c u", u=2),
                in_=bank[:].rearrange("p u c -> p c u"),
            )

        def quantise_last(i):
            last_codes[i] = keep.tile([P, P], U32, name="last_codes%d" % i, align_bytes=256)
            last_scales[i] = keep.tile([P, P], U8, name="last_scales%d" % i, align_bytes=256)
            quantise(last_grouped[i], last_codes[i][:], last_scales[i][:])

        def second_stage(n, i):
            rows = slice(i * P, (i + 1) * P)
            for chunk in range(2 * n, min(2 * n + 2, CHUNKS)):
                a_cols = slice((chunk - 2 * n) * CHUNK, (chunk - 2 * n + 1) * CHUNK)
                y = psum.tile([P, CHUNK], F32, tag="bank", name="y")
                for g2 in range(RANK_PASSES):
                    nc.tensor.matmul_mx(
                        out=y[:],
                        lhsT=zr_codes(n, g2, i).bitcast(FP8X4),
                        lhsT_scale=zr_scales(n, g2, i),
                        rhs=a_codes[:, g2, a_cols].bitcast(FP8X4),
                        rhs_scale=a_scales[:, g2, a_cols],
                        start=(g2 == 0),
                        stop=(g2 == RANK_PASSES - 1),
                    )
                cols = slice(chunk * CHUNK, (chunk + 1) * CHUNK)
                nc.vector.tensor_add(out=h_tok[:, i, cols], in0=y[:], in1=h_tok[:, i, cols])
                nc.sync.dma_start(out=out_rows[rows, cols], in_=h_tok[:, i, cols])

        x_grouped, w_grouped, a_grouped = {}, {}, {}
        w_codes, w_scales = {}, {}
        h_t, z_rot, products, regrouped = {}, {}, {}, {}

        def quantise_unit(unit):
            if unit < PASSES:
                quantise(x_grouped[unit], x_codes[:, unit, :], x_scales[:, unit, :])
            w_codes[unit] = unit_pool.tile([P, CHUNK], U32, tag="codes", name="w_codes", align_bytes=256)
            w_scales[unit] = unit_pool.tile([P, CHUNK], U8, tag="scales", name="w_scales", align_bytes=256)
            quantise(w_grouped[unit], w_codes[unit][:], w_scales[unit][:])

        def turn_unit(unit, engines):
            if unit < PASSES:
                x_grouped[unit] = transpose_unit(x_raw[unit], HX)
            w_grouped[unit] = transpose_unit(w_raw[unit], HW if unit < PASSES else engines)
            if unit + LOAD_AHEAD < UNITS:
                w_raw[unit + LOAD_AHEAD] = load_weight_unit(unit + LOAD_AHEAD)

        def load_lora(v):
            a_raw[v] = load_lora_unit(v // 2, v % 2)

        def turn_lora(v):
            a_grouped[v] = transpose_unit(a_raw[v], "SS")

        def quantise_lora(v):
            a_cols = slice(v % 2 * CHUNK, (v % 2 + 1) * CHUNK)
            quantise(a_grouped[v], a_codes[:, v // 2, a_cols], a_scales[:, v // 2, a_cols])

        due = {}

        def at(k, step, f, *arguments):
            due.setdefault((k, step), []).append((f, arguments))

        def run(k, step):
            for f, arguments in due.get((k, step), []):
                f(*arguments)

        def finish_slot(time, t, k):
            keep_slot(time, t, "V" if t % 2 == 1 and time in KV else "S")
            chunk = chunk_at(time)
            when = k + 1 if time else k + 1 + t // 2
            if time < 3 or t < 4 - LATE:
                at(when, "vector", rotate_slot, chunk, t)
            if t == PACK - 1 and time < 3:
                last = when
                at(last + 1, "vector", regroup_rotated, chunk)
                at(last + 2, "vector", quantise_rotated, chunk)
                for i in range(TOKEN_TILES):
                    at(k + 1 + HD + i // HP, "turn", transpose_h, chunk, i)

        for v in range(4):
            at(LL[v], "load", load_lora, v)
            at(LT[v], "turn", turn_lora, v)
            at(LT[v] + 1, "vector", quantise_lora, v)
        k = 0
        fresh = []
        for units, passes in HEAD:
            run(k, "load")
            for unit in units:
                turn_unit(unit, HE)
                if unit < EARLY:
                    quantise_unit(unit)
            for unit in fresh:
                if unit >= EARLY:
                    quantise_unit(unit)
            fresh = units
            run(k, "vector")
            run(k, "turn")
            for g in passes:
                for t in range(PACK):
                    first_stage_pass(0, t, g)
                if g == PASSES - 1:
                    for t in range(PACK):
                        finish_slot(0, t, k)
            k += 1
        turned = 2 * PASSES
        for time in range(1, CHUNKS - 1):
            for r in range(ROUNDS):
                run(k, "load")
                many = SHARE[time][r]
                units = range(turned, turned + many)
                turned += many
                for unit in units:
                    turn_unit(unit, VE[time])
                for unit in fresh:
                    quantise_unit(unit)
                fresh = units
                run(k, "vector")
                run(k, "turn")
                for t in range(r * PACK // ROUNDS, (r + 1) * PACK // ROUNDS):
                    for g in range(PASSES):
                        first_stage_pass(time, t, g)
                    finish_slot(time, t, k)
                run(k, "passes")
                if time == CHUNKS - 2:
                    for i in range(r * TOKEN_TILES // ROUNDS, (r + 1) * TOKEN_TILES // ROUNDS):
                        second_stage(1, i)
                k += 1

        before = chunk_at(CHUNKS - 2)
        for unit in fresh:
            quantise_unit(unit)
        run(k, "vector")
        for t in range(4 - LATE, 4):
            rotate_slot(before, t)
        last_chunk(0)
        last_chunk(1)
        transpose_h(before, 0)
        transpose_h(before, 1)
        transpose_last(0)
        regroup_rotated(before)
        last_chunk(2)
        transpose_h(before, 2)
        transpose_h(before, 3)
        transpose_last(1)
        keep_last(0)
        quantise_last(0)
        last_chunk(3)
        quantise_rotated(before)
        quantise_last(1)
        transpose_last(2)
        keep_last(1)
        second_stage(0, 0)
        second_stage(2, 0)
        quantise_last(2)
        second_stage(0, 1)
        transpose_last(3)
        keep_last(2)
        keep_last(3)
        second_stage(2, 1)
        quantise_last(3)
        second_stage(2, 2)
        second_stage(0, 2)
        second_stage(2, 3)
        second_stage(0, 3)
